import numpy as np
import ml_dtypes

BF16 = ml_dtypes.bfloat16


def bf(x):
    return np.asarray(x, np.float32).astype(BF16)


def f32(x):
    return np.asarray(x, np.float32)


def f64(x):
    return np.asarray(x).astype(np.float64)


def striped(idx):
    return np.tile(idx.reshape(-1, 16).T, (8, 1))


S, F, M, K, T, H, N = 2048, 128, 128, 2, 2, 1024, 8192


def setup_inputs():
    z = bf(np.random.standard_normal((F, S)))
    wsv = bf(np.random.standard_normal((F, M)) / np.sqrt(F))
    wsr = bf(np.random.standard_normal((F, M)) / np.sqrt(F))
    wdr = bf(np.random.standard_normal((F, M)) / np.sqrt(F))
    idx = np.concatenate([np.random.permutation(S)[:H] for _ in range(N // H)])
    return {"z": z, "wsv": wsv, "wsr": wsr, "wdr": wdr, "offs": striped(idx)}


def reference(z, wsv, wsr, wdr, offs):
    idx = offs[:16].T.reshape(-1)
    nb = idx.reshape(T, K, S)
    zz = f64(z)
    agg_s = np.zeros((M, S), np.float64)
    agg_d = np.zeros((M, S), np.float64)
    for k in range(K):
        agg_s = agg_s + f64(wsr).T @ zz[:, nb[0, k]]
        agg_d = agg_d + f64(wdr).T @ zz[:, nb[1, k]]
    node = f64(wsv).T @ zz
    return np.maximum(node + agg_s / K + agg_d / K, 0.0)

@@ -1,0 +1,53 @@
+import concourse.mybir as mybir
+
+BF16, F32, U16 = mybir.dt.bfloat16, mybir.dt.float32, mybir.dt.uint16
+
+FEATURES = 128
+FILTERS = 128
+NODES = 2048
+SLOTS = 2
+TYPES = 2
+BLOCK = 512
+BLOCKS = NODES // BLOCK
+LIST = TYPES * SLOTS * NODES
+PER_COLUMN = 16
+
+FLOPS = 2 * FEATURES * FILTERS * NODES * (1 + TYPES * SLOTS)
+
+
+def tile_gnn_layer_kernel(tc, z, wsv, wsr, wdr, offs, out):
+    nc = tc.nc
+    with (
+        tc.tile_pool(name="held", bufs=1) as held,
+        tc.psum_pool(name="psum", bufs=1) as psum,
+    ):
+        offsets = held.tile([128, LIST // PER_COLUMN], U16, name="offsets")
+        nc.sync.dma_start(offsets[:], offs)
+        table = held.tile([FEATURES, NODES], BF16, name="table")
+        nc.scalar.dma_start(table[:], z)
+        own = held.tile([FEATURES, FILTERS], BF16, name="own")
+        nc.sync.dma_start(own[:], wsv)
+
+        halved = []
+        for name, weights in (("same", wsr), ("diff", wdr)):
+            loaded = held.tile([FEATURES, FILTERS], BF16, name=name + "_loaded")
+            nc.sync.dma_start(loaded[:], weights)
+            half = held.tile([FEATURES, FILTERS], BF16, name=name + "_half")
+            nc.vector.tensor_scalar_mul(half[:], loaded[:], 0.5)
+            halved.append(half)
+
+        banks = [psum.tile([FILTERS, BLOCK], F32, name=f"bank{b}") for b in range(BLOCKS)]
+        for b in range(BLOCKS):
+            nc.tensor.matmul(banks[b][:], own[:], table[:, b * BLOCK : (b + 1) * BLOCK], start=True, stop=False)
+
+        result = held.tile([FILTERS, NODES], F32, name="result")
+        for b in range(BLOCKS):
+            for t in range(TYPES):
+                for k in range(SLOTS):
+                    first = ((t * SLOTS + k) * NODES + b * BLOCK) // PER_COLUMN
+                    piece = offsets[:, first : first + BLOCK // PER_COLUMN]
+                    last = t == TYPES - 1 and k == SLOTS - 1
+                    nc.tensor.matmul(banks[b][:], halved[t][:], table[:].indirect(piece), start=False, stop=last)
+            block = slice(b * BLOCK, (b + 1) * BLOCK)
+            nc.vector.tensor_scalar_max(result[:, block], banks[b][:], 0.0)
+            nc.sync.dma_start(out[:, block], result[:, block])

@@ -21,20 +21,23 @@ def tile_gnn_layer_kernel(tc, z, wsv, wsr, wdr, offs, out):
         tc.tile_pool(name="held", bufs=1) as held,
         tc.psum_pool(name="psum", bufs=1) as psum,
     ):
-        offsets = held.tile([128, LIST // PER_COLUMN], U16, name="offsets")
-        nc.sync.dma_start(offsets[:], offs)
-        table = held.tile([FEATURES, NODES], BF16, name="table")
-        nc.scalar.dma_start(table[:], z)
         own = held.tile([FEATURES, FILTERS], BF16, name="own")
         nc.sync.dma_start(own[:], wsv)
 
         halved = []
         for name, weights in (("same", wsr), ("diff", wdr)):
             loaded = held.tile([FEATURES, FILTERS], BF16, name=name + "_loaded")
-            nc.sync.dma_start(loaded[:], weights)
+            nc.scalar.dma_start(loaded[:], weights)
             half = held.tile([FEATURES, FILTERS], BF16, name=name + "_half")
             nc.vector.tensor_scalar_mul(half[:], loaded[:], 0.5)
             halved.append(half)
+
+        table = held.tile([FEATURES, NODES], BF16, name="table")
+        for b in range(BLOCKS):
+            queue = nc.sync if b % 2 == 0 else nc.scalar
+            queue.dma_start(table[:, b * BLOCK : (b + 1) * BLOCK], z[:, b * BLOCK : (b + 1) * BLOCK])
+        offsets = held.tile([128, LIST // PER_COLUMN], U16, name="offsets")
+        nc.sync.dma_start(offsets[:], offs)
 
         banks = [psum.tile([FILTERS, BLOCK], F32, name=f"bank{b}") for b in range(BLOCKS)]
         for b in range(BLOCKS):

@@ -11,6 +11,7 @@ BLOCK = 512
 BLOCKS = NODES // BLOCK
 LIST = TYPES * SLOTS * NODES
 PER_COLUMN = 16
+WARM_UP = 6
 
 FLOPS = 2 * FEATURES * FILTERS * NODES * (1 + TYPES * SLOTS)
 
@@ -21,6 +22,12 @@ def tile_gnn_layer_kernel(tc, z, wsv, wsr, wdr, offs, out):
         tc.tile_pool(name="held", bufs=1) as held,
         tc.psum_pool(name="psum", bufs=1) as psum,
     ):
+        zeros = held.tile([FEATURES, BLOCK], BF16, name="zeros")
+        nc.vector.memset(zeros[:], 0.0)
+        spare = psum.tile([FILTERS, BLOCK], F32, name="spare")
+        for w in range(WARM_UP):
+            nc.tensor.matmul(spare[:], zeros[:, :FILTERS], zeros[:], start=True, stop=True)
+
         own = held.tile([FEATURES, FILTERS], BF16, name="own")
         nc.sync.dma_start(own[:], wsv)
 

@@ -11,7 +11,7 @@ BLOCK = 512
 BLOCKS = NODES // BLOCK
 LIST = TYPES * SLOTS * NODES
 PER_COLUMN = 16
-WARM_UP = 6
+WARM_UP = 16
 
 FLOPS = 2 * FEATURES * FILTERS * NODES * (1 + TYPES * SLOTS)
 
@@ -22,11 +22,11 @@ def tile_gnn_layer_kernel(tc, z, wsv, wsr, wdr, offs, out):
         tc.tile_pool(name="held", bufs=1) as held,
         tc.psum_pool(name="psum", bufs=1) as psum,
     ):
-        zeros = held.tile([FEATURES, BLOCK], BF16, name="zeros")
+        zeros = held.tile([FEATURES, FILTERS], BF16, name="zeros")
         nc.vector.memset(zeros[:], 0.0)
-        spare = psum.tile([FILTERS, BLOCK], F32, name="spare")
+        spare = psum.tile([FILTERS, FILTERS], F32, name="spare")
         for w in range(WARM_UP):
-            nc.tensor.matmul(spare[:], zeros[:, :FILTERS], zeros[:], start=True, stop=True)
+            nc.tensor.matmul(spare[:], zeros[:], zeros[:], start=True, stop=True)
 
         own = held.tile([FEATURES, FILTERS], BF16, name="own")
         nc.sync.dma_start(own[:], wsv)

@@ -9,6 +9,7 @@ SLOTS = 2
 TYPES = 2
 BLOCK = 512
 BLOCKS = NODES // BLOCK
+HALF = BLOCK // 2
 LIST = TYPES * SLOTS * NODES
 PER_COLUMN = 16
 WARM_UP = 16
@@ -35,9 +36,9 @@ def tile_gnn_layer_kernel(tc, z, wsv, wsr, wdr, offs, out):
         for name, weights in (("same", wsr), ("diff", wdr)):
             loaded = held.tile([FEATURES, FILTERS], BF16, name=name + "_loaded")
             nc.scalar.dma_start(loaded[:], weights)
-            half = held.tile([FEATURES, FILTERS], BF16, name=name + "_half")
-            nc.vector.tensor_scalar_mul(half[:], loaded[:], 0.5)
-            halved.append(half)
+            scaled = held.tile([FEATURES, FILTERS], BF16, name=name + "_scaled")
+            nc.vector.tensor_scalar_mul(scaled[:], loaded[:], 0.5)
+            halved.append(scaled)
 
         table = held.tile([FEATURES, NODES], BF16, name="table")
         for b in range(BLOCKS):
@@ -58,6 +59,7 @@ def tile_gnn_layer_kernel(tc, z, wsv, wsr, wdr, offs, out):
                     piece = offsets[:, first : first + BLOCK // PER_COLUMN]
                     last = t == TYPES - 1 and k == SLOTS - 1
                     nc.tensor.matmul(banks[b][:], halved[t][:], table[:].indirect(piece), start=False, stop=last)
-            block = slice(b * BLOCK, (b + 1) * BLOCK)
-            nc.vector.tensor_scalar_max(result[:, block], banks[b][:], 0.0)
-            nc.sync.dma_start(out[:, block], result[:, block])
+            for h, queue in enumerate((nc.sync, nc.scalar)):
+                half = slice(b * BLOCK + h * HALF, b * BLOCK + (h + 1) * HALF)
+                nc.vector.tensor_scalar_max(result[:, half], banks[b][:, h * HALF : (h + 1) * HALF], 0.0)
+                queue.dma_start(out[:, half], result[:, half])

@@ -1,6 +1,7 @@
 import concourse.mybir as mybir
 
 BF16, F32, U16 = mybir.dt.bfloat16, mybir.dt.float32, mybir.dt.uint16
+MULT, MAX = mybir.AluOpType.mult, mybir.AluOpType.max
 
 FEATURES = 128
 FILTERS = 128
@@ -31,14 +32,13 @@ def tile_gnn_layer_kernel(tc, z, wsv, wsr, wdr, offs, out):
 
         own = held.tile([FEATURES, FILTERS], BF16, name="own")
         nc.sync.dma_start(own[:], wsv)
-
-        halved = []
+        doubled = held.tile([FEATURES, FILTERS], BF16, name="doubled")
+        nc.vector.tensor_scalar_mul(doubled[:], own[:], 2.0)
+        neighbour = []
         for name, weights in (("same", wsr), ("diff", wdr)):
-            loaded = held.tile([FEATURES, FILTERS], BF16, name=name + "_loaded")
+            loaded = held.tile([FEATURES, FILTERS], BF16, name=name)
             nc.scalar.dma_start(loaded[:], weights)
-            scaled = held.tile([FEATURES, FILTERS], BF16, name=name + "_scaled")
-            nc.vector.tensor_scalar_mul(scaled[:], loaded[:], 0.5)
-            halved.append(scaled)
+            neighbour.append(loaded)
 
         table = held.tile([FEATURES, NODES], BF16, name="table")
         for b in range(BLOCKS):
@@ -49,7 +49,7 @@ def tile_gnn_layer_kernel(tc, z, wsv, wsr, wdr, offs, out):
 
         banks = [psum.tile([FILTERS, BLOCK], F32, name=f"bank{b}") for b in range(BLOCKS)]
         for b in range(BLOCKS):
-            nc.tensor.matmul(banks[b][:], own[:], table[:, b * BLOCK : (b + 1) * BLOCK], start=True, stop=False)
+            nc.tensor.matmul(banks[b][:], doubled[:], table[:, b * BLOCK : (b + 1) * BLOCK], start=True, stop=False)
 
         result = held.tile([FILTERS, NODES], F32, name="result")
         for b in range(BLOCKS):
@@ -58,8 +58,8 @@ def tile_gnn_layer_kernel(tc, z, wsv, wsr, wdr, offs, out):
                     first = ((t * SLOTS + k) * NODES + b * BLOCK) // PER_COLUMN
                     piece = offsets[:, first : first + BLOCK // PER_COLUMN]
                     last = t == TYPES - 1 and k == SLOTS - 1
-                    nc.tensor.matmul(banks[b][:], halved[t][:], table[:].indirect(piece), start=False, stop=last)
+                    nc.tensor.matmul(banks[b][:], neighbour[t][:], table[:].indirect(piece), start=False, stop=last)
             for h, queue in enumerate((nc.sync, nc.scalar)):
                 half = slice(b * BLOCK + h * HALF, b * BLOCK + (h + 1) * HALF)
-                nc.vector.tensor_scalar_max(result[:, half], banks[b][:, h * HALF : (h + 1) * HALF], 0.0)
+                nc.vector.tensor_scalar(result[:, half], banks[b][:, h * HALF : (h + 1) * HALF], 0.5, 0.0, MULT, MAX)
                 queue.dma_start(out[:, half], result[:, half])

@@ -39,11 +39,9 @@ def tile_gnn_layer_kernel(tc, z, wsv, wsr, wdr, offs, out):
             loaded = held.tile([FEATURES, FILTERS], BF16, name=name)
             nc.scalar.dma_start(loaded[:], weights)
             neighbour.append(loaded)
-
         table = held.tile([FEATURES, NODES], BF16, name="table")
         for b in range(BLOCKS):
-            queue = nc.sync if b % 2 == 0 else nc.scalar
-            queue.dma_start(table[:, b * BLOCK : (b + 1) * BLOCK], z[:, b * BLOCK : (b + 1) * BLOCK])
+            nc.sync.dma_start(table[:, b * BLOCK : (b + 1) * BLOCK], z[:, b * BLOCK : (b + 1) * BLOCK])
         offsets = held.tile([128, LIST // PER_COLUMN], U16, name="offsets")
         nc.sync.dma_start(offsets[:], offs)
 

@@ -11,6 +11,7 @@ TYPES = 2
 BLOCK = 512
 BLOCKS = NODES // BLOCK
 HALF = BLOCK // 2
+LOAD = NODES // 2
 LIST = TYPES * SLOTS * NODES
 PER_COLUMN = 16
 WARM_UP = 16
@@ -40,8 +41,8 @@ def tile_gnn_layer_kernel(tc, z, wsv, wsr, wdr, offs, out):
             nc.scalar.dma_start(loaded[:], weights)
             neighbour.append(loaded)
         table = held.tile([FEATURES, NODES], BF16, name="table")
-        for b in range(BLOCKS):
-            nc.sync.dma_start(table[:, b * BLOCK : (b + 1) * BLOCK], z[:, b * BLOCK : (b + 1) * BLOCK])
+        for part in range(NODES // LOAD):
+            nc.sync.dma_start(table[:, part * LOAD : (part + 1) * LOAD], z[:, part * LOAD : (part + 1) * LOAD])
         offsets = held.tile([128, LIST // PER_COLUMN], U16, name="offsets")
         nc.sync.dma_start(offsets[:], offs)
 

@@ -61,4 +61,7 @@ def tile_gnn_layer_kernel(tc, z, wsv, wsr, wdr, offs, out):
             for h, queue in enumerate((nc.sync, nc.scalar)):
                 half = slice(b * BLOCK + h * HALF, b * BLOCK + (h + 1) * HALF)
                 nc.vector.tensor_scalar(result[:, half], banks[b][:, h * HALF : (h + 1) * HALF], 0.5, 0.0, MULT, MAX)
-                queue.dma_start(out[:, half], result[:, half])
+                if b == BLOCKS - 1:
+                    queue.dma_start(out[:, half], result[:, half])
+            if b == BLOCKS - 2:
+                nc.sync.dma_start(out[:, : (BLOCKS - 1) * BLOCK], result[:, : (BLOCKS - 1) * BLOCK])

import concourse.mybir as mybir

BF16, F32, U16 = mybir.dt.bfloat16, mybir.dt.float32, mybir.dt.uint16
MULT, MAX = mybir.AluOpType.mult, mybir.AluOpType.max

FEATURES = 128
FILTERS = 128
NODES = 2048
SLOTS = 2
TYPES = 2
BLOCK = 512
BLOCKS = NODES // BLOCK
HALF = BLOCK // 2
LOAD = NODES // 2
LIST = TYPES * SLOTS * NODES
PER_COLUMN = 16
WARM_UP = 16

FLOPS = 2 * FEATURES * FILTERS * NODES * (1 + TYPES * SLOTS)


def tile_gnn_layer_kernel(tc, z, wsv, wsr, wdr, offs, out):
    nc = tc.nc
    with (
        tc.tile_pool(name="held", bufs=1) as held,
        tc.psum_pool(name="psum", bufs=1) as psum,
    ):
        zeros = held.tile([FEATURES, FILTERS], BF16, name="zeros")
        nc.vector.memset(zeros[:], 0.0)
        spare = psum.tile([FILTERS, FILTERS], F32, name="spare")
        for w in range(WARM_UP):
            nc.tensor.matmul(spare[:], zeros[:], zeros[:], start=True, stop=True)

        own = held.tile([FEATURES, FILTERS], BF16, name="own")
        nc.sync.dma_start(own[:], wsv)
        doubled = held.tile([FEATURES, FILTERS], BF16, name="doubled")
        nc.vector.tensor_scalar_mul(doubled[:], own[:], 2.0)
        neighbour = []
        for name, weights in (("same", wsr), ("diff", wdr)):
            loaded = held.tile([FEATURES, FILTERS], BF16, name=name)
            nc.scalar.dma_start(loaded[:], weights)
            neighbour.append(loaded)
        table = held.tile([FEATURES, NODES], BF16, name="table")
        for part in range(NODES // LOAD):
            nc.sync.dma_start(table[:, part * LOAD : (part + 1) * LOAD], z[:, part * LOAD : (part + 1) * LOAD])
        offsets = held.tile([128, LIST // PER_COLUMN], U16, name="offsets")
        nc.sync.dma_start(offsets[:], offs)

        banks = [psum.tile([FILTERS, BLOCK], F32, name=f"bank{b}") for b in range(BLOCKS)]
        for b in range(BLOCKS):
            nc.tensor.matmul(banks[b][:], doubled[:], table[:, b * BLOCK : (b + 1) * BLOCK], start=True, stop=False)

        result = held.tile([FILTERS, NODES], F32, name="result")
        for b in range(BLOCKS):
            for t in range(TYPES):
                for k in range(SLOTS):
                    first = ((t * SLOTS + k) * NODES + b * BLOCK) // PER_COLUMN
                    piece = offsets[:, first : first + BLOCK // PER_COLUMN]
                    last = t == TYPES - 1 and k == SLOTS - 1
                    nc.tensor.matmul(banks[b][:], neighbour[t][:], table[:].indirect(piece), start=False, stop=last)
            for h, queue in enumerate((nc.sync, nc.scalar)):
                half = slice(b * BLOCK + h * HALF, b * BLOCK + (h + 1) * HALF)
                nc.vector.tensor_scalar(result[:, half], banks[b][:, h * HALF : (h + 1) * HALF], 0.5, 0.0, MULT, MAX)
                if b == BLOCKS - 1:
                    queue.dma_start(out[:, half], result[:, half])
            if b == BLOCKS - 2:
                nc.sync.dma_start(out[:, : (BLOCKS - 1) * BLOCK], result[:, : (BLOCKS - 1) * BLOCK])
